import numpy as np
import ml_dtypes


def mxq(x, axis, fmt="e4m3"):
    dtype, down = {"e4m3": (ml_dtypes.float8_e4m3fn, 7), "e5m2": (ml_dtypes.float8_e5m2, 14)}[fmt]
    v = np.moveaxis(np.asarray(x, np.float32).astype(ml_dtypes.bfloat16).astype(np.float64), axis, -1)
    blocks = v.reshape(v.shape[:-1] + (-1, 32))
    amax = np.abs(blocks).max(-1, keepdims=True)
    byte = np.maximum(np.where(amax > 0, np.frexp(amax)[1] - 1 + 127, 0) - down, 1)
    scale = np.exp2(byte - 127.0)
    codes = (blocks / scale).astype(np.float32).astype(dtype).astype(np.float64)
    return np.moveaxis((codes * scale).reshape(v.shape), -1, axis)


WIDE = False


def mx_kscale(k):
    if not WIDE:
        return np.ones(k)
    levels = np.array([10, -10, 5, -5, 0])
    a = np.random.permutation(np.resize(levels, k // 512 * 4)).reshape(k // 512, 4)
    idx = np.arange(k)
    return np.exp2(a[idx // 512, idx % 128 // 32])


BF16 = ml_dtypes.bfloat16


def bf(x):
    return np.asarray(x, np.float32).astype(BF16)


def f64(x):
    return np.asarray(x).astype(np.float64)


B, H, N, D = 2, 2, 1024, 512
LOG100 = np.log(100.0)


def unit(x):
    return x / np.sqrt((x * x).sum(-1, keepdims=True))


def setup_inputs():
    logit_scale = LOG100 + np.linspace(-3.0, 1.0, H) + 0.1 * np.random.standard_normal(H)
    soft = np.exp(np.minimum(logit_scale, LOG100)) / np.sqrt(D) < 1.8
    t = np.where(soft[:, None], mx_kscale(N)[None, :], 1.0)
    return {"q_hat": bf(unit(np.random.standard_normal((B, H, N, D)))),
            "k_hat": bf(unit(np.random.standard_normal((B, H, N, D)))),
            "v": bf(np.random.standard_normal((B, H, N, D)) * (t.mean(1, keepdims=True) / t)[None, :, :, None]),
            "logit_scale": bf(logit_scale.reshape(H, 1, 1)),
            "bias": bf(np.random.standard_normal((H, N, N)) + np.log(t)[:, None, :])}


def reference(q_hat, k_hat, v, logit_scale, bias):
    scores = f64(q_hat) @ f64(k_hat).transpose(0, 1, 3, 2)
    scale = np.exp(np.minimum(f64(logit_scale), LOG100))
    scores = scores * scale[None] + f64(bias)[None]
    e = np.exp(scores - scores.max(-1, keepdims=True))
    x = (mxq(e, 3, "e4m3") @ mxq(f64(v), 2, "e4m3")) / e.sum(-1, keepdims=True)
    return x.transpose(0, 2, 1, 3).reshape(B, -1, N * D)

@@ -1,0 +1,357 @@
+from contextlib import ExitStack
+
+import concourse.mybir as mybir
+from concourse.masks import make_identity
+
+F32 = mybir.dt.float32
+BF16 = mybir.dt.bfloat16
+U32 = mybir.dt.uint32
+U8 = mybir.dt.uint8
+FP8X4 = mybir.dt.float8_e4m3fn_x4
+ALU = mybir.AluOpType
+ACT = mybir.ActivationFunctionType
+AXIS = mybir.AxisListType
+
+NB, NH, N, D = 2, 2, 1024, 512
+P = 128
+QT = N // P
+DC = D // P
+HALF = 512
+HEADS = [(0, 0), (1, 0), (0, 1), (1, 1)]
+NTILES = len(HEADS) * QT
+FLOPS = 2 * 2 * NB * NH * N * N * D
+
+LT = 2
+LP = 4
+UNIT_ENGINE = "VSVSVSVS"
+PRO_ENGINE = "VSVSV"
+D_ENGINE = "SSSSSSSS"
+H_ENGINE = "SSSSSSSS"
+V_REGROUP = "G"
+PIN = True
+WB = 4
+
+
+def tile_attention_pa_t_kernel(tc, q_hat, k_hat, v, logit_scale, bias, out):
+    nc = tc.nc
+    q_rows = q_hat.rearrange("b h n d -> (b h n) d")
+    k_rows = k_hat.rearrange("b h n d -> (b h n) d")
+    v_rows = v.rearrange("b h n d -> (b h n) d")
+    bias_rows = bias.rearrange("h q k -> (h q) k")
+    out_rows = out.rearrange("b x (n h d) -> (b x n) h d", h=NH, d=D)
+
+    with ExitStack() as ctx:
+        const = ctx.enter_context(tc.tile_pool(name="const", bufs=1))
+        raw = ctx.enter_context(tc.tile_pool(name="raw", bufs=3))
+        tp = ctx.enter_context(tc.tile_pool(name="tp", bufs=2))
+        vq = ctx.enter_context(tc.tile_pool(name="vq", bufs=2))
+        work = ctx.enter_context(tc.tile_pool(name="work", bufs=WB))
+        small = ctx.enter_context(tc.tile_pool(name="small", bufs=6))
+        pss = ctx.enter_context(tc.psum_pool(name="pss", bufs=4))
+        psx = ctx.enter_context(tc.psum_pool(name="psx", bufs=3))
+        pso = ctx.enter_context(tc.psum_pool(name="pso", bufs=1))
+        if PIN:
+            ctx.enter_context(tc.manual_schedule())
+
+        q_raw, k_raw, v_raw, q_t, k_t, v_w, v_p, bias_sb = {}, {}, {}, {}, {}, {}, {}, {}
+        s_ps, nt_sb, negm, rsum, e_sb, x_ps, grp, e_w, e_p, o_ps = {}, {}, {}, {}, {}, {}, {}, {}, {}, {}
+
+        def row0(hd):
+            b, h = HEADS[hd]
+            return (b * NH + h) * N
+
+        def load_blocks(dst, rows, r0, t0, nt):
+            nc.sync.dma_start(
+                out=dst[:, t0 : t0 + nt, :],
+                in_=rows[r0 + t0 * P : r0 + (t0 + nt) * P, :].rearrange("(t p) d -> p t d", p=P),
+            )
+
+        def copy_out(eng, dst, src):
+            if eng == "V":
+                nc.vector.tensor_copy(out=dst, in_=src)
+            else:
+                nc.scalar.copy(out=dst, in_=src)
+
+        def load_q(hd, t0=0, nt=QT):
+            if t0 == 0:
+                q_raw[hd] = raw.tile([P, QT, D], BF16, name="q_raw")
+            load_blocks(q_raw[hd], q_rows, row0(hd), t0, nt)
+
+        def load_k(hd, t0=0, nt=QT):
+            if t0 == 0:
+                k_raw[hd] = raw.tile([P, QT, D], BF16, name="k_raw")
+            load_blocks(k_raw[hd], k_rows, row0(hd), t0, nt)
+
+        def load_v(hd):
+            v_raw[hd] = raw.tile([P, QT, D], BF16, name="v_raw", bufs=2)
+            load_blocks(v_raw[hd], v_rows, row0(hd), 0, QT)
+
+        def alloc_t(hd):
+            q_t[hd] = tp.tile([P, QT, DC, P], BF16, name="q_t")
+            k_t[hd] = tp.tile([P, DC, N], BF16, name="k_t")
+
+        def k_unit(hd, hf, cp):
+            x = psx.tile([P, 2, 4, P], BF16, name="xk", tag="x")
+            ops = []
+            for c2 in range(2):
+                for t4 in range(4):
+                    ops.append(
+                        lambda c2=c2, t4=t4: nc.tensor.transpose(
+                            x[:, c2, t4, :],
+                            k_raw[hd][:, 4 * hf + t4, (2 * cp + c2) * P : (2 * cp + c2 + 1) * P],
+                            ident[:],
+                        )
+                    )
+
+            def empty(eng):
+                copy_out(
+                    eng,
+                    k_t[hd][:, 2 * cp : 2 * cp + 2, hf * HALF : (hf + 1) * HALF],
+                    x[:].rearrange("p c t k -> p c (t k)"),
+                )
+
+            return ops, empty
+
+        def q_unit(hd, pr):
+            x = psx.tile([P, 2, DC, P], BF16, name="xq", tag="x")
+            ops = []
+            for i2 in range(2):
+                for c in range(DC):
+                    ops.append(
+                        lambda i2=i2, c=c: nc.tensor.transpose(
+                            x[:, i2, c, :], q_raw[hd][:, 2 * pr + i2, c * P : (c + 1) * P], ident[:]
+                        )
+                    )
+
+            def empty(eng):
+                copy_out(eng, q_t[hd][:, 2 * pr : 2 * pr + 2, :, :], x[:])
+
+            return ops, empty
+
+        def v_regroup(hd, g):
+            if g == 0:
+                grp_v[hd] = vq.tile([P, 2, D, 4], BF16, name="v_grp", bufs=1, align_bytes=64)
+            dst = grp_v[hd][:, g, :, :]
+            src = v_raw[hd][:, 4 * g : 4 * g + 4, :].rearrange("p t d -> p d t")
+            if V_REGROUP == "G":
+                nc.gpsimd.tensor_scalar(out=dst, in0=src, scalar1=1.0, scalar2=0.0, op0=ALU.mult, op1=ALU.add)
+            else:
+                nc.vector.tensor_copy(out=dst, in_=src)
+
+        def v_quant(hd):
+            v_w[hd] = vq.tile([P, 2, D], U32, name="v_w", align_bytes=64)
+            v_p[hd] = vq.tile([P, 2, D], U8, name="v_p", align_bytes=64)
+            nc.vector.quantize_mx(
+                out=v_w[hd][:].rearrange("p g d -> p (g d)").bitcast(FP8X4),
+                scales=v_p[hd][:].rearrange("p g d -> p (g d)"),
+                in_=grp_v[hd][:].rearrange("p g d t -> p (g d t)"),
+            )
+
+        grp_v = {}
+
+        def mm_ops(j):
+            hd, i = divmod(j, QT)
+            s_ps[j] = [pss.tile([P, HALF], F32, name="s", tag="s") for hf in range(2)]
+            ops = []
+            for hf in range(2):
+                for c in range(DC):
+                    ops.append(
+                        lambda hf=hf, c=c: nc.tensor.matmul(
+                            s_ps[j][hf][:],
+                            lhsT=q_t[hd][:, i, c, :],
+                            rhs=k_t[hd][:, c, hf * HALF : (hf + 1) * HALF],
+                            start=(c == 0),
+                            stop=(c == DC - 1),
+                        )
+                    )
+            return ops
+
+        def add_bias(j, hf):
+            hd, i = divmod(j, QT)
+            h = HEADS[hd][1]
+            if hf == 0:
+                nt_sb[j] = work.tile([P, N], F32, name="nt")
+            nc.vector.scalar_tensor_tensor(
+                out=nt_sb[j][:, hf * HALF : (hf + 1) * HALF],
+                in0=s_ps[j][hf][:],
+                scalar=negscale[:, h : h + 1],
+                in1=bias_sb[h][:, i, hf * HALF : (hf + 1) * HALF],
+                op0=ALU.mult,
+                op1=ALU.subtract,
+            )
+
+        def row_max(j):
+            negm[j] = small.tile([P, 1], F32, name="negm")
+            nc.vector.tensor_reduce(out=negm[j][:], in_=nt_sb[j][:], axis=AXIS.X, op=ALU.min)
+
+        def exp_(j):
+            e_sb[j] = work.tile([P, N], BF16, name="e")
+            rsum[j] = small.tile([P, 1], F32, name="rsum")
+            nc.scalar.activation(
+                out=e_sb[j][:], in_=nt_sb[j][:], func=ACT.Exp, bias=negm[j][:], scale=-1.0, accum_out=rsum[j][:]
+            )
+
+        def tr_ops(j):
+            x_ps[j] = psx.tile([P, 8, P], BF16, name="xe", tag="x")
+            return [
+                lambda kt=kt: nc.tensor.transpose(x_ps[j][:, kt, :], e_sb[j][:, kt * P : (kt + 1) * P], ident[:])
+                for kt in range(8)
+            ]
+
+        def regroup(j, eng):
+            grp[j] = work.tile([P, 2, P, 4], BF16, name="grp", align_bytes=64)
+            copy_out(eng, grp[j][:], x_ps[j][:].rearrange("p (g t) q -> p g q t", t=4))
+
+        def quant(j):
+            e_w[j] = work.tile([P, 2 * P], U32, name="e_w", align_bytes=64)
+            e_p[j] = work.tile([P, 2 * P], U8, name="e_p", align_bytes=64)
+            nc.vector.quantize_mx(
+                out=e_w[j][:].bitcast(FP8X4), scales=e_p[j][:], in_=grp[j][:].rearrange("p g q t -> p (g q t)")
+            )
+
+        def pv_ops(j):
+            hd = j // QT
+            o_ps[j] = pso.tile([P, D], F32, name="o")
+            return [
+                lambda g=g: nc.tensor.matmul_mx(
+                    out=o_ps[j][:],
+                    lhsT=e_w[j][:, g * P : (g + 1) * P].bitcast(FP8X4),
+                    lhsT_scale=e_p[j][:, g * P : (g + 1) * P],
+                    rhs=v_w[hd][:, g, :].bitcast(FP8X4),
+                    rhs_scale=v_p[hd][:, g, :],
+                    start=(g == 0),
+                    stop=(g == 1),
+                )
+                for g in range(2)
+            ]
+
+        def recip(j):
+            rinv[j] = small.tile([P, 1], F32, name="rinv")
+            nc.vector.reciprocal(out=rinv[j][:], in_=rsum[j][:])
+
+        def finish(j, eng):
+            hd, i = divmod(j, QT)
+            b, h = HEADS[hd]
+            o_sb = work.tile([P, D], F32, name="o_sb")
+            if eng == "V":
+                nc.vector.tensor_scalar(out=o_sb[:], in0=o_ps[j][:], scalar1=rinv[j][:], scalar2=None, op0=ALU.mult)
+            else:
+                nc.scalar.activation(out=o_sb[:], in_=o_ps[j][:], func=ACT.Copy, scale=rinv[j][:])
+            r0 = b * N + i * P
+            nc.sync.dma_start(
+                out=out_rows[r0 : r0 + P, h : h + 1, :], in_=o_sb[:].rearrange("p (o d) -> p o d", o=1)
+            )
+
+        rinv = {}
+
+        ident = const.tile([P, P], BF16, name="ident")
+        make_identity(nc, ident[:])
+        ls_bf = const.tile([P, NH], BF16, name="ls_bf")
+        nc.sync.dma_start(out=ls_bf[:], in_=logit_scale.rearrange("h a b -> (h a b)").partition_broadcast(P))
+        for h in range(NH):
+            bias_sb[h] = const.tile([P, QT, N], BF16, name="bias%d" % h)
+        load_k(0, 0, 4)
+        load_q(0, 0, 2)
+        load_k(0, 4, 4)
+        load_blocks(bias_sb[0], bias_rows, 0, 0, 2)
+        load_q(0, 2, 6)
+        load_blocks(bias_sb[0], bias_rows, 0, 2, 2)
+        load_v(0)
+        load_blocks(bias_sb[0], bias_rows, 0, 4, 4)
+        load_k(1)
+        load_q(1)
+        load_v(1)
+        load_blocks(bias_sb[1], bias_rows, N, 0, 8)
+        load_k(2)
+        load_q(2)
+
+        exp_ls = const.tile([P, NH], F32, name="exp_ls")
+        nc.scalar.activation(out=exp_ls[:], in_=ls_bf[:], func=ACT.Exp)
+        negscale = const.tile([P, NH], F32, name="negscale")
+        nc.vector.tensor_scalar(
+            out=negscale[:], in0=exp_ls[:], scalar1=100.0, scalar2=-1.0, op0=ALU.min, op1=ALU.mult
+        )
+
+        alloc_t(0)
+        first = [k_unit(0, 0, 0), k_unit(0, 0, 1), q_unit(0, 0)]
+        for n, (ops, empty) in enumerate(first):
+            for op in ops:
+                op()
+            empty(PRO_ENGINE[n])
+        for n, args in enumerate([(0, 1, 0), (0, 1, 1)]):
+            ops, empty = k_unit(*args)
+            for op in ops:
+                op()
+            empty(PRO_ENGINE[3 + n])
+        v_regroup(0, 0)
+        v_regroup(0, 1)
+
+        UNITS = ["q1", "q2", "q3", "k00", "k01", "q0", "k10", "k11"]
+
+        def make_unit(hd, i):
+            u = UNITS[i]
+            if i < 3:
+                return q_unit(hd, int(u[1]))
+            if hd + 1 == len(HEADS):
+                return None
+            if i == 3:
+                alloc_t(hd + 1)
+            if u[0] == "q":
+                return q_unit(hd + 1, int(u[1]))
+            return k_unit(hd + 1, int(u[1]), int(u[2]))
+
+        for j in range(NTILES + LP + 1):
+            hd, i = divmod(j, QT)
+            mm = mm_ops(j) if j < NTILES else []
+            tr = tr_ops(j - LT) if 0 <= j - LT < NTILES else []
+            unit = make_unit(hd, i) if j < NTILES else None
+            un = unit[0] if unit else []
+            pv = pv_ops(j - LP) if 0 <= j - LP < NTILES else []
+
+            for n in range(4):
+                if mm:
+                    mm[n]()
+                for op in tr[2 * n : 2 * n + 2]:
+                    op()
+            if mm:
+                add_bias(j, 0)
+                mm[4]()
+            for op in pv:
+                op()
+            for n in range(5, 8):
+                if mm:
+                    mm[n]()
+                for op in un[3 * (n - 5) : 3 * (n - 5) + 3]:
+                    op()
+            if 0 <= j - 1 < NTILES:
+                exp_(j - 1)
+            if mm:
+                add_bias(j, 1)
+            if pv:
+                finish(j - LP, H_ENGINE[i])
+            if tr:
+                regroup(j - LT, D_ENGINE[i])
+            if mm:
+                row_max(j)
+            if 0 <= j - 1 < NTILES:
+                recip(j - 1)
+            if tr:
+                quant(j - LT)
+            if unit:
+                unit[1](UNIT_ENGINE[i])
+            if j == 2:
+                v_quant(0)
+            if j < NTILES and hd + 1 < len(HEADS):
+                if i == 3:
+                    v_regroup(hd + 1, 0)
+                if i == 4:
+                    v_regroup(hd + 1, 1)
+                if i == 6:
+                    v_quant(hd + 1)
+            if j == 1:
+                load_k(3)
+                load_v(2)
+            if j == 4:
+                load_q(3)
+            if j == 6:
+                load_v(3)

@@ -30,6 +30,7 @@ H_ENGINE = "SSSSSSSS"
 V_REGROUP = "G"
 PIN = True
 WB = 4
+UCUT = [0, 2, 3, 4]
 
 
 def tile_attention_pa_t_kernel(tc, q_hat, k_hat, v, logit_scale, bias, out):
@@ -87,39 +88,31 @@ def tile_attention_pa_t_kernel(tc, q_hat, k_hat, v, logit_scale, bias, out):
             load_blocks(v_raw[hd], v_rows, row0(hd), 0, QT)
 
         def alloc_t(hd):
-            q_t[hd] = tp.tile([P, QT, DC, P], BF16, name="q_t")
-            k_t[hd] = tp.tile([P, DC, N], BF16, name="k_t")
+            q_t[hd] = tp.tile([P, QT, 2, P], F32, name="q_t")
+            k_t[hd] = tp.tile([P, 2, N], F32, name="k_t")
 
-        def k_unit(hd, hf, cp):
-            x = psx.tile([P, 2, 4, P], BF16, name="xk", tag="x")
-            ops = []
-            for c2 in range(2):
-                for t4 in range(4):
-                    ops.append(
-                        lambda c2=c2, t4=t4: nc.tensor.transpose(
-                            x[:, c2, t4, :],
-                            k_raw[hd][:, 4 * hf + t4, (2 * cp + c2) * P : (2 * cp + c2 + 1) * P],
-                            ident[:],
-                        )
-                    )
+        def k_unit(hd, hf, u):
+            x = psx.tile([P, 4, P], F32, name="xk", tag="x")
+            ops = [
+                lambda t4=t4: nc.tensor.transpose(
+                    x[:, t4, :], k_raw[hd][:, 4 * hf + t4, 2 * u * P : 2 * (u + 1) * P].bitcast(F32), ident32[:]
+                )
+                for t4 in range(4)
+            ]
 
             def empty(eng):
-                copy_out(
-                    eng,
-                    k_t[hd][:, 2 * cp : 2 * cp + 2, hf * HALF : (hf + 1) * HALF],
-                    x[:].rearrange("p c t k -> p c (t k)"),
-                )
+                copy_out(eng, k_t[hd][:, u, hf * HALF : (hf + 1) * HALF], x[:].rearrange("p t k -> p (t k)"))
 
             return ops, empty
 
         def q_unit(hd, pr):
-            x = psx.tile([P, 2, DC, P], BF16, name="xq", tag="x")
+            x = psx.tile([P, 2, 2, P], F32, name="xq", tag="x")
             ops = []
             for i2 in range(2):
-                for c in range(DC):
+                for u in range(2):
                     ops.append(
-                        lambda i2=i2, c=c: nc.tensor.transpose(
-                            x[:, i2, c, :], q_raw[hd][:, 2 * pr + i2, c * P : (c + 1) * P], ident[:]
+                        lambda i2=i2, u=u: nc.tensor.transpose(
+                            x[:, i2, u, :], q_raw[hd][:, 2 * pr + i2, 2 * u * P : 2 * (u + 1) * P].bitcast(F32), ident32[:]
                         )
                     )
 
@@ -158,8 +151,10 @@ def tile_attention_pa_t_kernel(tc, q_hat, k_hat, v, logit_scale, bias, out):
                     ops.append(
                         lambda hf=hf, c=c: nc.tensor.matmul(
                             s_ps[j][hf][:],
-                            lhsT=q_t[hd][:, i, c, :],
-                            rhs=k_t[hd][:, c, hf * HALF : (hf + 1) * HALF],
+                            lhsT=q_t[hd][:, i, c // 2, :].bitcast(BF16).rearrange("p (q e) -> p q e", e=2)[:, :, c % 2],
+                            rhs=k_t[hd][:, c // 2, hf * HALF : (hf + 1) * HALF]
+                            .bitcast(BF16)
+                            .rearrange("p (n e) -> p n e", e=2)[:, :, c % 2],
                             start=(c == 0),
                             stop=(c == DC - 1),
                         )
@@ -246,6 +241,8 @@ def tile_attention_pa_t_kernel(tc, q_hat, k_hat, v, logit_scale, bias, out):
 
         ident = const.tile([P, P], BF16, name="ident")
         make_identity(nc, ident[:])
+        ident32 = const.tile([P, P], F32, name="ident32")
+        make_identity(nc, ident32[:])
         ls_bf = const.tile([P, NH], BF16, name="ls_bf")
         nc.sync.dma_start(out=ls_bf[:], in_=logit_scale.rearrange("h a b -> (h a b)").partition_broadcast(P))
         for h in range(NH):
@@ -321,7 +318,7 @@ def tile_attention_pa_t_kernel(tc, q_hat, k_hat, v, logit_scale, bias, out):
             for n in range(5, 8):
                 if mm:
                     mm[n]()
-                for op in un[3 * (n - 5) : 3 * (n - 5) + 3]:
+                for op in un[UCUT[n - 5] : UCUT[n - 4]]:
                     op()
             if 0 <= j - 1 < NTILES:
                 exp_(j - 1)

@@ -24,13 +24,34 @@ FLOPS = 2 * 2 * NB * NH * N * N * D
 LT = 2
 LP = 4
 UNIT_ENGINE = "VSVSVSVS"
-PRO_ENGINE = "VSVSV"
+PRO_ENGINE = "VSVSVS"
+PRO_UNITS = ["k00", "k01", "q0", "k10", "k11"]
+UNITS = ["q1", "q2", "q3", "K00", "K01", "Q0", "K10", "K11"]
 D_ENGINE = "SSSSSSSS"
 H_ENGINE = "SSSSSSSS"
 V_REGROUP = "G"
 PIN = True
 WB = 4
-UCUT = [0, 2, 3, 4]
+VPIECES = 8
+FIRST_UNITS = ["q1", "q2", "q3", "K00", "K01+Q0", "K10", "K11", "Q1"]
+LATER_LOADS = {0: [("k", 1), ("q", 1)], 2: [("v", 1)], 6: [("b", 1)], 8: [("k", 2), ("q", 2)], 10: [("v", 2)], 16: [("k", 3), ("q", 3)], 18: [("v", 3)]}
+SCHED = []
+VQ0 = 2
+ORDER = [
+    ("M", 0), ("T", 2, 0, 2), ("M", 1), ("T", 2, 2, 4), ("M", 2), ("T", 2, 4, 6), ("M", 3), ("T", 2, 6, 8),
+    ("A", 0), ("M", 4), ("X", 4), ("M", 5), ("U", 0, 2), ("M", 6), ("U", 2, 3), ("M", 7), ("U", 3, 4),
+    ("C", 1), ("A", 1), ("H", 4), ("D", 2), ("B",), ("R", 1), ("E", 2), ("UE", 0),
+]
+
+
+ORDER = [["M",0],["T",2,0,2],["M",1],["T",2,2,4],["M",2],["T",2,4,6],["M",3],["T",2,6,8],["M",4],["U",0,2],["M",5],["U",2,3],["M",6],["U",3,4],["M",7],["X",4],["UE",1],["A",0],["E",3],["A",1],["B"],["R",2],["C",1],["D",2],["H",5]]
+UNITS = [["q2"],["q3"],["K00"],["K01"],["Q0"],["K10"],["K11"],["Q1"]]
+PRO_UNITS = ["k00","k01","q0","k10","k11"]
+FIRST_UNITS = [["q1"],["q2"],["q3"],["K00"],["K01","Q0"],["K10"],["K11"],["Q1"]]
+VQ0 = 3
+UNIT_ENGINE = "SSSSSSSSVSVSVSVSSSVSVSVSVSVSVSVS"
+D_ENGINE = "SSSSSSSSSSSSSSSSSSSSSSSSSSSSSSSS"
+H_ENGINE = "VSSSSVSSSSSVSVSSSSSVSVSVSVSVVSSS"
 
 
 def tile_attention_pa_t_kernel(tc, q_hat, k_hat, v, logit_scale, bias, out):
@@ -47,7 +68,7 @@ def tile_attention_pa_t_kernel(tc, q_hat, k_hat, v, logit_scale, bias, out):
         tp = ctx.enter_context(tc.tile_pool(name="tp", bufs=2))
         vq = ctx.enter_context(tc.tile_pool(name="vq", bufs=2))
         work = ctx.enter_context(tc.tile_pool(name="work", bufs=WB))
-        small = ctx.enter_context(tc.tile_pool(name="small", bufs=6))
+        small = ctx.enter_context(tc.tile_pool(name="small", bufs=10))
         pss = ctx.enter_context(tc.psum_pool(name="pss", bufs=4))
         psx = ctx.enter_context(tc.psum_pool(name="psx", bufs=3))
         pso = ctx.enter_context(tc.psum_pool(name="pso", bufs=1))
@@ -121,15 +142,15 @@ def tile_attention_pa_t_kernel(tc, q_hat, k_hat, v, logit_scale, bias, out):
 
             return ops, empty
 
-        def v_regroup(hd, g):
-            if g == 0:
+        def v_regroup(hd, piece):
+            if piece == 0:
                 grp_v[hd] = vq.tile([P, 2, D, 4], BF16, name="v_grp", bufs=1, align_bytes=64)
-            dst = grp_v[hd][:, g, :, :]
-            src = v_raw[hd][:, 4 * g : 4 * g + 4, :].rearrange("p t d -> p d t")
-            if V_REGROUP == "G":
-                nc.gpsimd.tensor_scalar(out=dst, in0=src, scalar1=1.0, scalar2=0.0, op0=ALU.mult, op1=ALU.add)
-            else:
-                nc.vector.tensor_copy(out=dst, in_=src)
+            per_g = VPIECES // 2
+            g, part = divmod(piece, per_g)
+            w = D // per_g
+            dst = grp_v[hd][:, g, part * w : (part + 1) * w, :]
+            src = v_raw[hd][:, 4 * g : 4 * g + 4, part * w : (part + 1) * w].rearrange("p t d -> p d t")
+            nc.gpsimd.tensor_scalar(out=dst, in0=src, scalar1=1.0, scalar2=0.0, op0=ALU.mult, op1=ALU.add)
 
         def v_quant(hd):
             v_w[hd] = vq.tile([P, 2, D], U32, name="v_w", align_bytes=64)
@@ -165,7 +186,7 @@ def tile_attention_pa_t_kernel(tc, q_hat, k_hat, v, logit_scale, bias, out):
             hd, i = divmod(j, QT)
             h = HEADS[hd][1]
             if hf == 0:
-                nt_sb[j] = work.tile([P, N], F32, name="nt")
+                nt_sb[j] = work.tile([P, N], F32, name="nt", bufs=5)
             nc.vector.scalar_tensor_tensor(
                 out=nt_sb[j][:, hf * HALF : (hf + 1) * HALF],
                 in0=s_ps[j][hf][:],
@@ -180,7 +201,7 @@ def tile_attention_pa_t_kernel(tc, q_hat, k_hat, v, logit_scale, bias, out):
             nc.vector.tensor_reduce(out=negm[j][:], in_=nt_sb[j][:], axis=AXIS.X, op=ALU.min)
 
         def exp_(j):
-            e_sb[j] = work.tile([P, N], BF16, name="e")
+            e_sb[j] = work.tile([P, N], BF16, name="e", bufs=6)
             rsum[j] = small.tile([P, 1], F32, name="rsum")
             nc.scalar.activation(
                 out=e_sb[j][:], in_=nt_sb[j][:], func=ACT.Exp, bias=negm[j][:], scale=-1.0, accum_out=rsum[j][:]
@@ -194,7 +215,7 @@ def tile_attention_pa_t_kernel(tc, q_hat, k_hat, v, logit_scale, bias, out):
             ]
 
         def regroup(j, eng):
-            grp[j] = work.tile([P, 2, P, 4], BF16, name="grp", align_bytes=64)
+            grp[j] = work.tile([P, 2, P, 4], BF16, name="grp", align_bytes=64, bufs=3)
             copy_out(eng, grp[j][:], x_ps[j][:].rearrange("p (g t) q -> p g q t", t=4))
 
         def quant(j):
@@ -239,6 +260,26 @@ def tile_attention_pa_t_kernel(tc, q_hat, k_hat, v, logit_scale, bias, out):
 
         rinv = {}
 
+        mm_cache = {}
+
+        def side_work(j):
+            hd, i = divmod(j, QT)
+            if j == 0:
+                for piece in range(VPIECES):
+                    v_regroup(0, piece)
+            for what, hd2 in LATER_LOADS.get(j, []):
+                if what == "k":
+                    load_k(hd2)
+                elif what == "q":
+                    load_q(hd2)
+                elif what == "v":
+                    load_v(hd2)
+                else:
+                    load_blocks(bias_sb[1], bias_rows, N, 0, 8)
+            if i == 3 and hd + 1 < len(HEADS):
+                for piece in range(VPIECES):
+                    v_regroup(hd + 1, piece)
+
         ident = const.tile([P, P], BF16, name="ident")
         make_identity(nc, ident[:])
         ident32 = const.tile([P, P], F32, name="ident32")
@@ -250,17 +291,13 @@ def tile_attention_pa_t_kernel(tc, q_hat, k_hat, v, logit_scale, bias, out):
         load_k(0, 0, 4)
         load_q(0, 0, 2)
         load_k(0, 4, 4)
-        load_blocks(bias_sb[0], bias_rows, 0, 0, 2)
-        load_q(0, 2, 6)
+        load_blocks(bias_sb[0], bias_rows, 0, 0, 1)
+        load_q(0, 2, 2)
+        load_blocks(bias_sb[0], bias_rows, 0, 1, 1)
+        load_q(0, 4, 4)
         load_blocks(bias_sb[0], bias_rows, 0, 2, 2)
         load_v(0)
         load_blocks(bias_sb[0], bias_rows, 0, 4, 4)
-        load_k(1)
-        load_q(1)
-        load_v(1)
-        load_blocks(bias_sb[1], bias_rows, N, 0, 8)
-        load_k(2)
-        load_q(2)
 
         exp_ls = const.tile([P, NH], F32, name="exp_ls")
         nc.scalar.activation(out=exp_ls[:], in_=ls_bf[:], func=ACT.Exp)
@@ -270,85 +307,101 @@ def tile_attention_pa_t_kernel(tc, q_hat, k_hat, v, logit_scale, bias, out):
         )
 
         alloc_t(0)
-        first = [k_unit(0, 0, 0), k_unit(0, 0, 1), q_unit(0, 0)]
-        for n, (ops, empty) in enumerate(first):
+        for n, u in enumerate(PRO_UNITS):
+            ops, empty = q_unit(0, int(u[1])) if u[0] == "q" else k_unit(0, int(u[1]), int(u[2]))
             for op in ops:
                 op()
             empty(PRO_ENGINE[n])
-        for n, args in enumerate([(0, 1, 0), (0, 1, 1)]):
-            ops, empty = k_unit(*args)
-            for op in ops:
-                op()
-            empty(PRO_ENGINE[3 + n])
-        v_regroup(0, 0)
-        v_regroup(0, 1)
 
-        UNITS = ["q1", "q2", "q3", "k00", "k01", "q0", "k10", "k11"]
-
-        def make_unit(hd, i):
-            u = UNITS[i]
-            if i < 3:
-                return q_unit(hd, int(u[1]))
-            if hd + 1 == len(HEADS):
+        def one_unit(hd, u):
+            nxt = u[0] in "KQ"
+            if nxt and hd + 1 == len(HEADS):
                 return None
-            if i == 3:
+            if nxt and hd + 1 not in q_t:
                 alloc_t(hd + 1)
-            if u[0] == "q":
-                return q_unit(hd + 1, int(u[1]))
+            if u[0] in "qQ":
+                return q_unit(hd + (1 if nxt else 0), int(u[1]))
             return k_unit(hd + 1, int(u[1]), int(u[2]))
 
-        for j in range(NTILES + LP + 1):
-            hd, i = divmod(j, QT)
-            mm = mm_ops(j) if j < NTILES else []
-            tr = tr_ops(j - LT) if 0 <= j - LT < NTILES else []
-            unit = make_unit(hd, i) if j < NTILES else None
-            un = unit[0] if unit else []
-            pv = pv_ops(j - LP) if 0 <= j - LP < NTILES else []
+        def make_unit(hd, i):
+            names = FIRST_UNITS[i] if hd == 0 else UNITS[i]
+            made = [m for m in [one_unit(hd, u) for u in names] if m]
+            if not made:
+                return None
+            ops = []
+            for m in made:
+                ops.extend(m[0])
 
-            for n in range(4):
-                if mm:
-                    mm[n]()
-                for op in tr[2 * n : 2 * n + 2]:
-                    op()
-            if mm:
-                add_bias(j, 0)
-                mm[4]()
-            for op in pv:
-                op()
-            for n in range(5, 8):
-                if mm:
-                    mm[n]()
-                for op in un[UCUT[n - 5] : UCUT[n - 4]]:
-                    op()
-            if 0 <= j - 1 < NTILES:
-                exp_(j - 1)
-            if mm:
-                add_bias(j, 1)
-            if pv:
-                finish(j - LP, H_ENGINE[i])
-            if tr:
-                regroup(j - LT, D_ENGINE[i])
-            if mm:
-                row_max(j)
-            if 0 <= j - 1 < NTILES:
-                recip(j - 1)
-            if tr:
-                quant(j - LT)
-            if unit:
-                unit[1](UNIT_ENGINE[i])
-            if j == 2:
+            def empty(engs):
+                for n, m in enumerate(made):
+                    m[1](engs[n % len(engs)])
+
+            return ops, empty
+
+        units = {}
+        cache = {}
+
+        def ok(t):
+            return 0 <= t < NTILES
+
+        maxlag = max(tok[1] for tok in ORDER if tok[0] in "TXCDERH")
+        for j in range(NTILES + maxlag + 1):
+            hd, i = divmod(j, QT)
+            if j < NTILES:
+                side_work(j)
+            for tok in ORDER:
+                kind = tok[0]
+                if kind == "M":
+                    if ok(j):
+                        if tok[1] == 0:
+                            cache["mm"] = mm_ops(j)
+                        cache["mm"][tok[1]]()
+                elif kind == "T":
+                    t = j - tok[1]
+                    if ok(t):
+                        if tok[2] == 0:
+                            cache["tr"] = tr_ops(t)
+                        for op in cache["tr"][tok[2] : tok[3]]:
+                            op()
+                elif kind == "U":
+                    if ok(j):
+                        if tok[1] == 0:
+                            units[j] = make_unit(hd, i)
+                        if units[j]:
+                            nu = len(units[j][0]) // 4
+                            for op in units[j][0][nu * tok[1] : nu * tok[2]]:
+                                op()
+                elif kind == "UE":
+                    t = j - tok[1]
+                    if ok(t) and units[t]:
+                        units[t][1](UNIT_ENGINE[t % len(UNIT_ENGINE)])
+                elif kind == "X":
+                    t = j - tok[1]
+                    if ok(t):
+                        for op in pv_ops(t):
+                            op()
+                elif kind == "A":
+                    if ok(j):
+                        add_bias(j, tok[1])
+                elif kind == "B":
+                    if ok(j):
+                        row_max(j)
+                elif kind == "C":
+                    if ok(j - tok[1]):
+                        exp_(j - tok[1])
+                elif kind == "D":
+                    if ok(j - tok[1]):
+                        regroup(j - tok[1], D_ENGINE[(j - tok[1]) % len(D_ENGINE)])
+                elif kind == "E":
+                    if ok(j - tok[1]):
+                        quant(j - tok[1])
+                elif kind == "R":
+                    if ok(j - tok[1]):
+                        recip(j - tok[1])
+                elif kind == "H":
+                    if ok(j - tok[1]):
+                        finish(j - tok[1], H_ENGINE[(j - tok[1]) % len(H_ENGINE)])
+            if j == VQ0:
                 v_quant(0)
-            if j < NTILES and hd + 1 < len(HEADS):
-                if i == 3:
-                    v_regroup(hd + 1, 0)
-                if i == 4:
-                    v_regroup(hd + 1, 1)
-                if i == 6:
-                    v_quant(hd + 1)
-            if j == 1:
-                load_k(3)
-                load_v(2)
-            if j == 4:
-                load_q(3)
-            if j == 6:
-                load_v(3)
+            if j < NTILES and i == 6 and hd + 1 < len(HEADS):
+                v_quant(hd + 1)

@@ -12,46 +12,27 @@ ALU = mybir.AluOpType
 ACT = mybir.ActivationFunctionType
 AXIS = mybir.AxisListType
 
-NB, NH, N, D = 2, 2, 1024, 512
+WINDOWS, NHEADS, N, D = 2, 2, 1024, 512
 P = 128
-QT = N // P
-DC = D // P
-HALF = 512
+TILES = N // P
+BANK = 512
+PACK = 4
+PASSES = N // (P * PACK)
 HEADS = [(0, 0), (1, 0), (0, 1), (1, 1)]
-NTILES = len(HEADS) * QT
-FLOPS = 2 * 2 * NB * NH * N * N * D
+ALL_TILES = len(HEADS) * TILES
+FLOPS = 2 * 2 * WINDOWS * NHEADS * N * N * D
 
-LT = 2
-LP = 4
-UNIT_ENGINE = "VSVSVSVS"
-PRO_ENGINE = "VSVSVS"
-PRO_UNITS = ["k00", "k01", "q0", "k10", "k11"]
-UNITS = ["q1", "q2", "q3", "K00", "K01", "Q0", "K10", "K11"]
-D_ENGINE = "SSSSSSSS"
-H_ENGINE = "SSSSSSSS"
-V_REGROUP = "G"
-PIN = True
-WB = 4
-VPIECES = 8
-FIRST_UNITS = ["q1", "q2", "q3", "K00", "K01+Q0", "K10", "K11", "Q1"]
-LATER_LOADS = {0: [("k", 1), ("q", 1)], 2: [("v", 1)], 6: [("b", 1)], 8: [("k", 2), ("q", 2)], 10: [("v", 2)], 16: [("k", 3), ("q", 3)], 18: [("v", 3)]}
-SCHED = []
-VQ0 = 2
-ORDER = [
-    ("M", 0), ("T", 2, 0, 2), ("M", 1), ("T", 2, 2, 4), ("M", 2), ("T", 2, 4, 6), ("M", 3), ("T", 2, 6, 8),
-    ("A", 0), ("M", 4), ("X", 4), ("M", 5), ("U", 0, 2), ("M", 6), ("U", 2, 3), ("M", 7), ("U", 3, 4),
-    ("C", 1), ("A", 1), ("H", 4), ("D", 2), ("B",), ("R", 1), ("E", 2), ("UE", 0),
-]
+EXP_LAG = 1
+TRANSPOSE_LAG = 2
+QUANTISE_LAG = 3
+MX_LAG = 4
 
+UNITS_BEFORE_A_HEAD = (0, 1, 4, 2, 3)
+UNITS_IN_A_HEAD = (5, 6, 7)
 
-ORDER = [["M",0],["T",2,0,2],["M",1],["T",2,2,4],["M",2],["T",2,4,6],["M",3],["T",2,6,8],["M",4],["U",0,2],["M",5],["U",2,3],["M",6],["U",3,4],["M",7],["X",4],["UE",1],["A",0],["E",3],["A",1],["B"],["R",2],["C",1],["D",2],["H",5]]
-UNITS = [["q2"],["q3"],["K00"],["K01"],["Q0"],["K10"],["K11"],["Q1"]]
-PRO_UNITS = ["k00","k01","q0","k10","k11"]
-FIRST_UNITS = [["q1"],["q2"],["q3"],["K00"],["K01","Q0"],["K10"],["K11"],["Q1"]]
-VQ0 = 3
-UNIT_ENGINE = "SSSSSSSSVSVSVSVSSSVSVSVSVSVSVSVS"
-D_ENGINE = "SSSSSSSSSSSSSSSSSSSSSSSSSSSSSSSS"
-H_ENGINE = "VSSSSVSSSSSVSVSSSSSVSVSVSVSVVSSS"
+V_PIECES = 8
+V_PIECES_A_STEP = 2
+V_FIRST_STEP = 3
 
 
 def tile_attention_pa_t_kernel(tc, q_hat, k_hat, v, logit_scale, bias, out):
@@ -60,348 +41,265 @@ def tile_attention_pa_t_kernel(tc, q_hat, k_hat, v, logit_scale, bias, out):
     k_rows = k_hat.rearrange("b h n d -> (b h n) d")
     v_rows = v.rearrange("b h n d -> (b h n) d")
     bias_rows = bias.rearrange("h q k -> (h q) k")
-    out_rows = out.rearrange("b x (n h d) -> (b x n) h d", h=NH, d=D)
+    out_rows = out.rearrange("b x (n h d) -> (b x n) h d", h=NHEADS, d=D)
 
     with ExitStack() as ctx:
         const = ctx.enter_context(tc.tile_pool(name="const", bufs=1))
-        raw = ctx.enter_context(tc.tile_pool(name="raw", bufs=3))
-        tp = ctx.enter_context(tc.tile_pool(name="tp", bufs=2))
-        vq = ctx.enter_context(tc.tile_pool(name="vq", bufs=2))
-        work = ctx.enter_context(tc.tile_pool(name="work", bufs=WB))
-        small = ctx.enter_context(tc.tile_pool(name="small", bufs=10))
-        pss = ctx.enter_context(tc.psum_pool(name="pss", bufs=4))
-        psx = ctx.enter_context(tc.psum_pool(name="psx", bufs=3))
-        pso = ctx.enter_context(tc.psum_pool(name="pso", bufs=1))
-        if PIN:
-            ctx.enter_context(tc.manual_schedule())
+        raw = ctx.enter_context(tc.tile_pool(name="raw", bufs=2))
+        operands = ctx.enter_context(tc.tile_pool(name="operands", bufs=2))
+        work = ctx.enter_context(tc.tile_pool(name="work", bufs=4))
+        columns = ctx.enter_context(tc.tile_pool(name="columns", bufs=8))
+        score_banks = ctx.enter_context(tc.psum_pool(name="score_banks", bufs=4))
+        transpose_banks = ctx.enter_context(tc.psum_pool(name="transpose_banks", bufs=3))
+        output_banks = ctx.enter_context(tc.psum_pool(name="output_banks", bufs=1))
+        ctx.enter_context(tc.manual_schedule())
 
-        q_raw, k_raw, v_raw, q_t, k_t, v_w, v_p, bias_sb = {}, {}, {}, {}, {}, {}, {}, {}
-        s_ps, nt_sb, negm, rsum, e_sb, x_ps, grp, e_w, e_p, o_ps = {}, {}, {}, {}, {}, {}, {}, {}, {}, {}
+        q_raw, k_raw, v_raw, q_t, k_t, v_grouped, v_words, v_scales, unit_bank = {}, {}, {}, {}, {}, {}, {}, {}, {}
+        score, neg_s, neg_max, row_sum, inv_sum, e_bf, e_bank, e_grouped, e_words, e_scales, x_bank = (
+            {}, {}, {}, {}, {}, {}, {}, {}, {}, {}, {},
+        )
 
-        def row0(hd):
-            b, h = HEADS[hd]
-            return (b * NH + h) * N
+        def first_row(head):
+            b, h = HEADS[head]
+            return (b * NHEADS + h) * N
 
-        def load_blocks(dst, rows, r0, t0, nt):
+        def load_blocks(dst, rows, row0, first, count):
             nc.sync.dma_start(
-                out=dst[:, t0 : t0 + nt, :],
-                in_=rows[r0 + t0 * P : r0 + (t0 + nt) * P, :].rearrange("(t p) d -> p t d", p=P),
+                out=dst[:, first : first + count, :],
+                in_=rows[row0 + first * P : row0 + (first + count) * P, :].rearrange("(t p) d -> p t d", p=P),
             )
 
-        def copy_out(eng, dst, src):
-            if eng == "V":
+        def new_head(head):
+            q_raw[head] = raw.tile([P, TILES, D], BF16, name="q_raw")
+            k_raw[head] = raw.tile([P, TILES, D], BF16, name="k_raw")
+            v_raw[head] = raw.tile([P, TILES, D], BF16, name="v_raw")
+            q_t[head] = operands.tile([P, TILES, 2, P], F32, name="q_t")
+            k_t[head] = operands.tile([P, 2, N], F32, name="k_t")
+
+        def unit_transposes(head, unit):
+            bank = transpose_banks.tile([P, 4, P], F32, name="unit_bank", tag="bank")
+            unit_bank[(head, unit)] = bank
+            for m in range(4):
+                if unit < 4:
+                    key_half, u = divmod(unit, 2)
+                    src = k_raw[head][:, 4 * key_half + m, 2 * u * P : 2 * (u + 1) * P]
+                else:
+                    tile_in_pair, u = divmod(m, 2)
+                    src = q_raw[head][:, 2 * (unit - 4) + tile_in_pair, 2 * u * P : 2 * (u + 1) * P]
+                nc.tensor.transpose(bank[:, m, :], src.bitcast(F32), identity_f32[:])
+
+        def unit_copy(head, unit, on_vector):
+            if unit < 4:
+                key_half, u = divmod(unit, 2)
+                dst = k_t[head][:, u, key_half * BANK : (key_half + 1) * BANK]
+            else:
+                dst = q_t[head][:, 2 * (unit - 4) : 2 * (unit - 3), :, :].rearrange("p i u q -> p (i u q)")
+            src = unit_bank[(head, unit)][:].rearrange("p m c -> p (m c)")
+            if on_vector:
                 nc.vector.tensor_copy(out=dst, in_=src)
             else:
                 nc.scalar.copy(out=dst, in_=src)
 
-        def load_q(hd, t0=0, nt=QT):
-            if t0 == 0:
-                q_raw[hd] = raw.tile([P, QT, D], BF16, name="q_raw")
-            load_blocks(q_raw[hd], q_rows, row0(hd), t0, nt)
-
-        def load_k(hd, t0=0, nt=QT):
-            if t0 == 0:
-                k_raw[hd] = raw.tile([P, QT, D], BF16, name="k_raw")
-            load_blocks(k_raw[hd], k_rows, row0(hd), t0, nt)
-
-        def load_v(hd):
-            v_raw[hd] = raw.tile([P, QT, D], BF16, name="v_raw", bufs=2)
-            load_blocks(v_raw[hd], v_rows, row0(hd), 0, QT)
-
-        def alloc_t(hd):
-            q_t[hd] = tp.tile([P, QT, 2, P], F32, name="q_t")
-            k_t[hd] = tp.tile([P, 2, N], F32, name="k_t")
-
-        def k_unit(hd, hf, u):
-            x = psx.tile([P, 4, P], F32, name="xk", tag="x")
-            ops = [
-                lambda t4=t4: nc.tensor.transpose(
-                    x[:, t4, :], k_raw[hd][:, 4 * hf + t4, 2 * u * P : 2 * (u + 1) * P].bitcast(F32), ident32[:]
-                )
-                for t4 in range(4)
-            ]
-
-            def empty(eng):
-                copy_out(eng, k_t[hd][:, u, hf * HALF : (hf + 1) * HALF], x[:].rearrange("p t k -> p (t k)"))
-
-            return ops, empty
-
-        def q_unit(hd, pr):
-            x = psx.tile([P, 2, 2, P], F32, name="xq", tag="x")
-            ops = []
-            for i2 in range(2):
-                for u in range(2):
-                    ops.append(
-                        lambda i2=i2, u=u: nc.tensor.transpose(
-                            x[:, i2, u, :], q_raw[hd][:, 2 * pr + i2, 2 * u * P : 2 * (u + 1) * P].bitcast(F32), ident32[:]
-                        )
-                    )
-
-            def empty(eng):
-                copy_out(eng, q_t[hd][:, 2 * pr : 2 * pr + 2, :, :], x[:])
-
-            return ops, empty
-
-        def v_regroup(hd, piece):
+        def regroup_v(head, piece):
             if piece == 0:
-                grp_v[hd] = vq.tile([P, 2, D, 4], BF16, name="v_grp", bufs=1, align_bytes=64)
-            per_g = VPIECES // 2
-            g, part = divmod(piece, per_g)
-            w = D // per_g
-            dst = grp_v[hd][:, g, part * w : (part + 1) * w, :]
-            src = v_raw[hd][:, 4 * g : 4 * g + 4, part * w : (part + 1) * w].rearrange("p t d -> p d t")
-            nc.gpsimd.tensor_scalar(out=dst, in0=src, scalar1=1.0, scalar2=0.0, op0=ALU.mult, op1=ALU.add)
-
-        def v_quant(hd):
-            v_w[hd] = vq.tile([P, 2, D], U32, name="v_w", align_bytes=64)
-            v_p[hd] = vq.tile([P, 2, D], U8, name="v_p", align_bytes=64)
-            nc.vector.quantize_mx(
-                out=v_w[hd][:].rearrange("p g d -> p (g d)").bitcast(FP8X4),
-                scales=v_p[hd][:].rearrange("p g d -> p (g d)"),
-                in_=grp_v[hd][:].rearrange("p g d t -> p (g d t)"),
+                v_grouped[head] = operands.tile([P, PASSES, D, PACK], BF16, name="v_grouped", bufs=1, align_bytes=64)
+            g, part = divmod(piece, V_PIECES // PASSES)
+            width = D * PASSES // V_PIECES
+            nc.gpsimd.tensor_scalar(
+                out=v_grouped[head][:, g, part * width : (part + 1) * width, :],
+                in0=v_raw[head][:, PACK * g : PACK * (g + 1), part * width : (part + 1) * width].rearrange(
+                    "p t d -> p d t"
+                ),
+                scalar1=1.0,
+                scalar2=0.0,
+                op0=ALU.mult,
+                op1=ALU.add,
             )
 
-        grp_v = {}
+        def quantise_v(head):
+            v_words[head] = operands.tile([P, PASSES, D], U32, name="v_words", align_bytes=64)
+            v_scales[head] = operands.tile([P, PASSES, D], U8, name="v_scales", align_bytes=64)
+            nc.vector.quantize_mx(
+                out=v_words[head][:].rearrange("p g d -> p (g d)").bitcast(FP8X4),
+                scales=v_scales[head][:].rearrange("p g d -> p (g d)"),
+                in_=v_grouped[head][:].rearrange("p g d t -> p (g d t)"),
+            )
 
-        def mm_ops(j):
-            hd, i = divmod(j, QT)
-            s_ps[j] = [pss.tile([P, HALF], F32, name="s", tag="s") for hf in range(2)]
-            ops = []
-            for hf in range(2):
-                for c in range(DC):
-                    ops.append(
-                        lambda hf=hf, c=c: nc.tensor.matmul(
-                            s_ps[j][hf][:],
-                            lhsT=q_t[hd][:, i, c // 2, :].bitcast(BF16).rearrange("p (q e) -> p q e", e=2)[:, :, c % 2],
-                            rhs=k_t[hd][:, c // 2, hf * HALF : (hf + 1) * HALF]
-                            .bitcast(BF16)
-                            .rearrange("p (n e) -> p n e", e=2)[:, :, c % 2],
-                            start=(c == 0),
-                            stop=(c == DC - 1),
-                        )
-                    )
-            return ops
+        def scores(j, key_half):
+            head, i = divmod(j, TILES)
+            score[(j, key_half)] = score_banks.tile([P, BANK], F32, name="score")
+            for c in range(4):
+                u, member = divmod(c, 2)
+                nc.tensor.matmul(
+                    score[(j, key_half)][:],
+                    lhsT=q_t[head][:, i, u, :].bitcast(BF16).rearrange("p (q e) -> p q e", e=2)[:, :, member],
+                    rhs=k_t[head][:, u, key_half * BANK : (key_half + 1) * BANK]
+                    .bitcast(BF16)
+                    .rearrange("p (n e) -> p n e", e=2)[:, :, member],
+                    start=(c == 0),
+                    stop=(c == 3),
+                )
 
-        def add_bias(j, hf):
-            hd, i = divmod(j, QT)
-            h = HEADS[hd][1]
-            if hf == 0:
-                nt_sb[j] = work.tile([P, N], F32, name="nt", bufs=5)
+        def add_bias(j, key_half):
+            head, i = divmod(j, TILES)
+            h = HEADS[head][1]
+            if key_half == 0:
+                neg_s[j] = work.tile([P, N], F32, name="neg_s")
+            keys = slice(key_half * BANK, (key_half + 1) * BANK)
             nc.vector.scalar_tensor_tensor(
-                out=nt_sb[j][:, hf * HALF : (hf + 1) * HALF],
-                in0=s_ps[j][hf][:],
-                scalar=negscale[:, h : h + 1],
-                in1=bias_sb[h][:, i, hf * HALF : (hf + 1) * HALF],
+                out=neg_s[j][:, keys],
+                in0=score[(j, key_half)][:],
+                scalar=neg_factor[:, h : h + 1],
+                in1=bias_sb[h][:, i, keys],
                 op0=ALU.mult,
                 op1=ALU.subtract,
             )
 
-        def row_max(j):
-            negm[j] = small.tile([P, 1], F32, name="negm")
-            nc.vector.tensor_reduce(out=negm[j][:], in_=nt_sb[j][:], axis=AXIS.X, op=ALU.min)
+        def row_maximum(j):
+            neg_max[j] = columns.tile([P, 1], F32, name="neg_max")
+            nc.vector.tensor_reduce(out=neg_max[j][:], in_=neg_s[j][:], axis=AXIS.X, op=ALU.min)
 
-        def exp_(j):
-            e_sb[j] = work.tile([P, N], BF16, name="e", bufs=6)
-            rsum[j] = small.tile([P, 1], F32, name="rsum")
+        def exponential(j):
+            e_bf[j] = work.tile([P, N], BF16, name="e_bf")
+            row_sum[j] = columns.tile([P, 1], F32, name="row_sum")
             nc.scalar.activation(
-                out=e_sb[j][:], in_=nt_sb[j][:], func=ACT.Exp, bias=negm[j][:], scale=-1.0, accum_out=rsum[j][:]
+                out=e_bf[j][:], in_=neg_s[j][:], func=ACT.Exp, bias=neg_max[j][:], scale=-1.0, accum_out=row_sum[j][:]
             )
 
-        def tr_ops(j):
-            x_ps[j] = psx.tile([P, 8, P], BF16, name="xe", tag="x")
-            return [
-                lambda kt=kt: nc.tensor.transpose(x_ps[j][:, kt, :], e_sb[j][:, kt * P : (kt + 1) * P], ident[:])
-                for kt in range(8)
-            ]
+        def transpose_e(j):
+            e_bank[j] = transpose_banks.tile([P, PASSES * PACK, P], BF16, name="e_bank", tag="bank")
+            for block in range(PASSES * PACK):
+                nc.tensor.transpose(e_bank[j][:, block, :], e_bf[j][:, block * P : (block + 1) * P], identity_bf16[:])
 
-        def regroup(j, eng):
-            grp[j] = work.tile([P, 2, P, 4], BF16, name="grp", align_bytes=64, bufs=3)
-            copy_out(eng, grp[j][:], x_ps[j][:].rearrange("p (g t) q -> p g q t", t=4))
+        def regroup_e(j):
+            e_grouped[j] = work.tile([P, PASSES, P, PACK], BF16, name="e_grouped", align_bytes=64)
+            nc.scalar.copy(out=e_grouped[j][:], in_=e_bank[j][:].rearrange("p (g t) q -> p g q t", t=PACK))
 
-        def quant(j):
-            e_w[j] = work.tile([P, 2 * P], U32, name="e_w", align_bytes=64)
-            e_p[j] = work.tile([P, 2 * P], U8, name="e_p", align_bytes=64)
+        def quantise_e(j):
+            e_words[j] = work.tile([P, PASSES * P], U32, name="e_words", align_bytes=64)
+            e_scales[j] = work.tile([P, PASSES * P], U8, name="e_scales", align_bytes=64)
             nc.vector.quantize_mx(
-                out=e_w[j][:].bitcast(FP8X4), scales=e_p[j][:], in_=grp[j][:].rearrange("p g q t -> p (g q t)")
+                out=e_words[j][:].bitcast(FP8X4),
+                scales=e_scales[j][:],
+                in_=e_grouped[j][:].rearrange("p g q t -> p (g q t)"),
             )
+            inv_sum[j] = columns.tile([P, 1], F32, name="inv_sum")
+            nc.vector.reciprocal(out=inv_sum[j][:], in_=row_sum[j][:])
 
-        def pv_ops(j):
-            hd = j // QT
-            o_ps[j] = pso.tile([P, D], F32, name="o")
-            return [
-                lambda g=g: nc.tensor.matmul_mx(
-                    out=o_ps[j][:],
-                    lhsT=e_w[j][:, g * P : (g + 1) * P].bitcast(FP8X4),
-                    lhsT_scale=e_p[j][:, g * P : (g + 1) * P],
-                    rhs=v_w[hd][:, g, :].bitcast(FP8X4),
-                    rhs_scale=v_p[hd][:, g, :],
+        def mx_passes(j):
+            head = j // TILES
+            x_bank[j] = output_banks.tile([P, D], F32, name="x_bank")
+            for g in range(PASSES):
+                queries = slice(g * P, (g + 1) * P)
+                nc.tensor.matmul_mx(
+                    out=x_bank[j][:],
+                    lhsT=e_words[j][:, queries].bitcast(FP8X4),
+                    lhsT_scale=e_scales[j][:, queries],
+                    rhs=v_words[head][:, g, :].bitcast(FP8X4),
+                    rhs_scale=v_scales[head][:, g, :],
                     start=(g == 0),
-                    stop=(g == 1),
+                    stop=(g == PASSES - 1),
                 )
-                for g in range(2)
-            ]
 
-        def recip(j):
-            rinv[j] = small.tile([P, 1], F32, name="rinv")
-            nc.vector.reciprocal(out=rinv[j][:], in_=rsum[j][:])
-
-        def finish(j, eng):
-            hd, i = divmod(j, QT)
-            b, h = HEADS[hd]
-            o_sb = work.tile([P, D], F32, name="o_sb")
-            if eng == "V":
-                nc.vector.tensor_scalar(out=o_sb[:], in0=o_ps[j][:], scalar1=rinv[j][:], scalar2=None, op0=ALU.mult)
-            else:
-                nc.scalar.activation(out=o_sb[:], in_=o_ps[j][:], func=ACT.Copy, scale=rinv[j][:])
-            r0 = b * N + i * P
+        def output(j):
+            head, i = divmod(j, TILES)
+            b, h = HEADS[head]
+            x_sb = work.tile([P, D], F32, name="x_sb")
+            nc.scalar.activation(out=x_sb[:], in_=x_bank[j][:], func=ACT.Copy, scale=inv_sum[j][:])
+            row0 = b * N + i * P
             nc.sync.dma_start(
-                out=out_rows[r0 : r0 + P, h : h + 1, :], in_=o_sb[:].rearrange("p (o d) -> p o d", o=1)
+                out=out_rows[row0 : row0 + P, h : h + 1, :], in_=x_sb[:].rearrange("p (o d) -> p o d", o=1)
             )
 
-        rinv = {}
-
-        mm_cache = {}
-
-        def side_work(j):
-            hd, i = divmod(j, QT)
-            if j == 0:
-                for piece in range(VPIECES):
-                    v_regroup(0, piece)
-            for what, hd2 in LATER_LOADS.get(j, []):
-                if what == "k":
-                    load_k(hd2)
-                elif what == "q":
-                    load_q(hd2)
-                elif what == "v":
-                    load_v(hd2)
-                else:
-                    load_blocks(bias_sb[1], bias_rows, N, 0, 8)
-            if i == 3 and hd + 1 < len(HEADS):
-                for piece in range(VPIECES):
-                    v_regroup(hd + 1, piece)
-
-        ident = const.tile([P, P], BF16, name="ident")
-        make_identity(nc, ident[:])
-        ident32 = const.tile([P, P], F32, name="ident32")
-        make_identity(nc, ident32[:])
-        ls_bf = const.tile([P, NH], BF16, name="ls_bf")
-        nc.sync.dma_start(out=ls_bf[:], in_=logit_scale.rearrange("h a b -> (h a b)").partition_broadcast(P))
-        for h in range(NH):
-            bias_sb[h] = const.tile([P, QT, N], BF16, name="bias%d" % h)
-        load_k(0, 0, 4)
-        load_q(0, 0, 2)
-        load_k(0, 4, 4)
+        identity_bf16 = const.tile([P, P], BF16, name="identity_bf16")
+        make_identity(nc, identity_bf16[:])
+        identity_f32 = const.tile([P, P], F32, name="identity_f32")
+        make_identity(nc, identity_f32[:])
+        log_factor = const.tile([P, NHEADS], BF16, name="log_factor")
+        nc.sync.dma_start(out=log_factor[:], in_=logit_scale.rearrange("h a b -> (h a b)").partition_broadcast(P))
+        bias_sb = [const.tile([P, TILES, N], BF16, name="bias%d" % h) for h in range(NHEADS)]
+        new_head(0)
+        load_blocks(k_raw[0], k_rows, first_row(0), 0, 4)
+        load_blocks(q_raw[0], q_rows, first_row(0), 0, 2)
+        load_blocks(k_raw[0], k_rows, first_row(0), 4, 4)
         load_blocks(bias_sb[0], bias_rows, 0, 0, 1)
-        load_q(0, 2, 2)
+        load_blocks(v_raw[0], v_rows, first_row(0), 0, TILES)
+        load_blocks(q_raw[0], q_rows, first_row(0), 2, 2)
         load_blocks(bias_sb[0], bias_rows, 0, 1, 1)
-        load_q(0, 4, 4)
+        load_blocks(q_raw[0], q_rows, first_row(0), 4, 4)
         load_blocks(bias_sb[0], bias_rows, 0, 2, 2)
-        load_v(0)
         load_blocks(bias_sb[0], bias_rows, 0, 4, 4)
 
-        exp_ls = const.tile([P, NH], F32, name="exp_ls")
-        nc.scalar.activation(out=exp_ls[:], in_=ls_bf[:], func=ACT.Exp)
-        negscale = const.tile([P, NH], F32, name="negscale")
+        factor = const.tile([P, NHEADS], F32, name="factor")
+        nc.scalar.activation(out=factor[:], in_=log_factor[:], func=ACT.Exp)
+        neg_factor = const.tile([P, NHEADS], F32, name="neg_factor")
         nc.vector.tensor_scalar(
-            out=negscale[:], in0=exp_ls[:], scalar1=100.0, scalar2=-1.0, op0=ALU.min, op1=ALU.mult
+            out=neg_factor[:], in0=factor[:], scalar1=100.0, scalar2=-1.0, op0=ALU.min, op1=ALU.mult
         )
 
-        alloc_t(0)
-        for n, u in enumerate(PRO_UNITS):
-            ops, empty = q_unit(0, int(u[1])) if u[0] == "q" else k_unit(0, int(u[1]), int(u[2]))
-            for op in ops:
-                op()
-            empty(PRO_ENGINE[n])
+        for position, unit in enumerate(UNITS_BEFORE_A_HEAD):
+            unit_transposes(0, unit)
+            unit_copy(0, unit, on_vector=(position % 2 == 0))
+        for piece in range(V_PIECES):
+            regroup_v(0, piece)
 
-        def one_unit(hd, u):
-            nxt = u[0] in "KQ"
-            if nxt and hd + 1 == len(HEADS):
-                return None
-            if nxt and hd + 1 not in q_t:
-                alloc_t(hd + 1)
-            if u[0] in "qQ":
-                return q_unit(hd + (1 if nxt else 0), int(u[1]))
-            return k_unit(hd + 1, int(u[1]), int(u[2]))
+        def is_tile(j):
+            return 0 <= j < ALL_TILES
 
-        def make_unit(hd, i):
-            names = FIRST_UNITS[i] if hd == 0 else UNITS[i]
-            made = [m for m in [one_unit(hd, u) for u in names] if m]
-            if not made:
-                return None
-            ops = []
-            for m in made:
-                ops.extend(m[0])
+        for step in range(ALL_TILES + MX_LAG):
+            head, i = divmod(step, TILES)
+            prepare = head + 1
+            preparing = is_tile(step) and prepare < len(HEADS)
 
-            def empty(engs):
-                for n, m in enumerate(made):
-                    m[1](engs[n % len(engs)])
+            if preparing and i == 0:
+                new_head(prepare)
+                load_blocks(k_raw[prepare], k_rows, first_row(prepare), 0, TILES)
+            if preparing and i == 1:
+                load_blocks(q_raw[prepare], q_rows, first_row(prepare), 0, TILES)
+            if preparing and i == 2:
+                load_blocks(v_raw[prepare], v_rows, first_row(prepare), 0, TILES)
+            if step == 3:
+                load_blocks(bias_sb[1], bias_rows, N, 0, TILES)
 
-            return ops, empty
+            if i < len(UNITS_IN_A_HEAD):
+                unit_head, unit = head, UNITS_IN_A_HEAD[i]
+            else:
+                unit_head, unit = prepare, UNITS_BEFORE_A_HEAD[i - len(UNITS_IN_A_HEAD)]
+            has_unit = is_tile(step) and unit_head < len(HEADS)
 
-        units = {}
-        cache = {}
+            if is_tile(step):
+                scores(step, 0)
+            if is_tile(step - MX_LAG):
+                mx_passes(step - MX_LAG)
+            if is_tile(step):
+                scores(step, 1)
+            if is_tile(step - TRANSPOSE_LAG):
+                transpose_e(step - TRANSPOSE_LAG)
+            if has_unit:
+                unit_transposes(unit_head, unit)
 
-        def ok(t):
-            return 0 <= t < NTILES
+            if is_tile(step):
+                add_bias(step, 0)
+            if is_tile(step - QUANTISE_LAG):
+                quantise_e(step - QUANTISE_LAG)
+            if is_tile(step):
+                add_bias(step, 1)
+                row_maximum(step)
+            if step == MX_LAG - 2:
+                quantise_v(0)
+            if preparing and i == TILES - 1:
+                quantise_v(prepare)
 
-        maxlag = max(tok[1] for tok in ORDER if tok[0] in "TXCDERH")
-        for j in range(NTILES + maxlag + 1):
-            hd, i = divmod(j, QT)
-            if j < NTILES:
-                side_work(j)
-            for tok in ORDER:
-                kind = tok[0]
-                if kind == "M":
-                    if ok(j):
-                        if tok[1] == 0:
-                            cache["mm"] = mm_ops(j)
-                        cache["mm"][tok[1]]()
-                elif kind == "T":
-                    t = j - tok[1]
-                    if ok(t):
-                        if tok[2] == 0:
-                            cache["tr"] = tr_ops(t)
-                        for op in cache["tr"][tok[2] : tok[3]]:
-                            op()
-                elif kind == "U":
-                    if ok(j):
-                        if tok[1] == 0:
-                            units[j] = make_unit(hd, i)
-                        if units[j]:
-                            nu = len(units[j][0]) // 4
-                            for op in units[j][0][nu * tok[1] : nu * tok[2]]:
-                                op()
-                elif kind == "UE":
-                    t = j - tok[1]
-                    if ok(t) and units[t]:
-                        units[t][1](UNIT_ENGINE[t % len(UNIT_ENGINE)])
-                elif kind == "X":
-                    t = j - tok[1]
-                    if ok(t):
-                        for op in pv_ops(t):
-                            op()
-                elif kind == "A":
-                    if ok(j):
-                        add_bias(j, tok[1])
-                elif kind == "B":
-                    if ok(j):
-                        row_max(j)
-                elif kind == "C":
-                    if ok(j - tok[1]):
-                        exp_(j - tok[1])
-                elif kind == "D":
-                    if ok(j - tok[1]):
-                        regroup(j - tok[1], D_ENGINE[(j - tok[1]) % len(D_ENGINE)])
-                elif kind == "E":
-                    if ok(j - tok[1]):
-                        quant(j - tok[1])
-                elif kind == "R":
-                    if ok(j - tok[1]):
-                        recip(j - tok[1])
-                elif kind == "H":
-                    if ok(j - tok[1]):
-                        finish(j - tok[1], H_ENGINE[(j - tok[1]) % len(H_ENGINE)])
-            if j == VQ0:
-                v_quant(0)
-            if j < NTILES and i == 6 and hd + 1 < len(HEADS):
-                v_quant(hd + 1)
+            if is_tile(step - EXP_LAG):
+                exponential(step - EXP_LAG)
+            if is_tile(step - MX_LAG):
+                output(step - MX_LAG)
+            if is_tile(step - TRANSPOSE_LAG):
+                regroup_e(step - TRANSPOSE_LAG)
+            if has_unit:
+                unit_copy(unit_head, unit, on_vector=False)
+
+            first_piece = (i - V_FIRST_STEP) * V_PIECES_A_STEP
+            if preparing and 0 <= first_piece < V_PIECES:
+                for piece in range(first_piece, first_piece + V_PIECES_A_STEP):
+                    regroup_v(prepare, piece)

from contextlib import ExitStack

import concourse.mybir as mybir
from concourse.masks import make_identity

F32 = mybir.dt.float32
BF16 = mybir.dt.bfloat16
U32 = mybir.dt.uint32
U8 = mybir.dt.uint8
FP8X4 = mybir.dt.float8_e4m3fn_x4
ALU = mybir.AluOpType
ACT = mybir.ActivationFunctionType
AXIS = mybir.AxisListType

WINDOWS, NHEADS, N, D = 2, 2, 1024, 512
P = 128
TILES = N // P
BANK = 512
PACK = 4
PASSES = N // (P * PACK)
HEADS = [(0, 0), (1, 0), (0, 1), (1, 1)]
ALL_TILES = len(HEADS) * TILES
FLOPS = 2 * 2 * WINDOWS * NHEADS * N * N * D

EXP_LAG = 1
TRANSPOSE_LAG = 2
QUANTISE_LAG = 3
MX_LAG = 4

UNITS_BEFORE_A_HEAD = (0, 1, 4, 2, 3)
UNITS_IN_A_HEAD = (5, 6, 7)

V_PIECES = 8
V_PIECES_A_STEP = 2
V_FIRST_STEP = 3


def tile_attention_pa_t_kernel(tc, q_hat, k_hat, v, logit_scale, bias, out):
    nc = tc.nc
    q_rows = q_hat.rearrange("b h n d -> (b h n) d")
    k_rows = k_hat.rearrange("b h n d -> (b h n) d")
    v_rows = v.rearrange("b h n d -> (b h n) d")
    bias_rows = bias.rearrange("h q k -> (h q) k")
    out_rows = out.rearrange("b x (n h d) -> (b x n) h d", h=NHEADS, d=D)

    with ExitStack() as ctx:
        const = ctx.enter_context(tc.tile_pool(name="const", bufs=1))
        raw = ctx.enter_context(tc.tile_pool(name="raw", bufs=2))
        operands = ctx.enter_context(tc.tile_pool(name="operands", bufs=2))
        work = ctx.enter_context(tc.tile_pool(name="work", bufs=4))
        columns = ctx.enter_context(tc.tile_pool(name="columns", bufs=8))
        score_banks = ctx.enter_context(tc.psum_pool(name="score_banks", bufs=4))
        transpose_banks = ctx.enter_context(tc.psum_pool(name="transpose_banks", bufs=3))
        output_banks = ctx.enter_context(tc.psum_pool(name="output_banks", bufs=1))
        ctx.enter_context(tc.manual_schedule())

        q_raw, k_raw, v_raw, q_t, k_t, v_grouped, v_words, v_scales, unit_bank = {}, {}, {}, {}, {}, {}, {}, {}, {}
        score, neg_s, neg_max, row_sum, inv_sum, e_bf, e_bank, e_grouped, e_words, e_scales, x_bank = (
            {}, {}, {}, {}, {}, {}, {}, {}, {}, {}, {},
        )

        def first_row(head):
            b, h = HEADS[head]
            return (b * NHEADS + h) * N

        def load_blocks(dst, rows, row0, first, count):
            nc.sync.dma_start(
                out=dst[:, first : first + count, :],
                in_=rows[row0 + first * P : row0 + (first + count) * P, :].rearrange("(t p) d -> p t d", p=P),
            )

        def new_head(head):
            q_raw[head] = raw.tile([P, TILES, D], BF16, name="q_raw")
            k_raw[head] = raw.tile([P, TILES, D], BF16, name="k_raw")
            v_raw[head] = raw.tile([P, TILES, D], BF16, name="v_raw")
            q_t[head] = operands.tile([P, TILES, 2, P], F32, name="q_t")
            k_t[head] = operands.tile([P, 2, N], F32, name="k_t")

        def unit_transposes(head, unit):
            bank = transpose_banks.tile([P, 4, P], F32, name="unit_bank", tag="bank")
            unit_bank[(head, unit)] = bank
            for m in range(4):
                if unit < 4:
                    key_half, u = divmod(unit, 2)
                    src = k_raw[head][:, 4 * key_half + m, 2 * u * P : 2 * (u + 1) * P]
                else:
                    tile_in_pair, u = divmod(m, 2)
                    src = q_raw[head][:, 2 * (unit - 4) + tile_in_pair, 2 * u * P : 2 * (u + 1) * P]
                nc.tensor.transpose(bank[:, m, :], src.bitcast(F32), identity_f32[:])

        def unit_copy(head, unit, on_vector):
            if unit < 4:
                key_half, u = divmod(unit, 2)
                dst = k_t[head][:, u, key_half * BANK : (key_half + 1) * BANK]
            else:
                dst = q_t[head][:, 2 * (unit - 4) : 2 * (unit - 3), :, :].rearrange("p i u q -> p (i u q)")
            src = unit_bank[(head, unit)][:].rearrange("p m c -> p (m c)")
            if on_vector:
                nc.vector.tensor_copy(out=dst, in_=src)
            else:
                nc.scalar.copy(out=dst, in_=src)

        def regroup_v(head, piece):
            if piece == 0:
                v_grouped[head] = operands.tile([P, PASSES, D, PACK], BF16, name="v_grouped", bufs=1, align_bytes=64)
            g, part = divmod(piece, V_PIECES // PASSES)
            width = D * PASSES // V_PIECES
            nc.gpsimd.tensor_scalar(
                out=v_grouped[head][:, g, part * width : (part + 1) * width, :],
                in0=v_raw[head][:, PACK * g : PACK * (g + 1), part * width : (part + 1) * width].rearrange(
                    "p t d -> p d t"
                ),
                scalar1=1.0,
                scalar2=0.0,
                op0=ALU.mult,
                op1=ALU.add,
            )

        def quantise_v(head):
            v_words[head] = operands.tile([P, PASSES, D], U32, name="v_words", align_bytes=64)
            v_scales[head] = operands.tile([P, PASSES, D], U8, name="v_scales", align_bytes=64)
            nc.vector.quantize_mx(
                out=v_words[head][:].rearrange("p g d -> p (g d)").bitcast(FP8X4),
                scales=v_scales[head][:].rearrange("p g d -> p (g d)"),
                in_=v_grouped[head][:].rearrange("p g d t -> p (g d t)"),
            )

        def scores(j, key_half):
            head, i = divmod(j, TILES)
            score[(j, key_half)] = score_banks.tile([P, BANK], F32, name="score")
            for c in range(4):
                u, member = divmod(c, 2)
                nc.tensor.matmul(
                    score[(j, key_half)][:],
                    lhsT=q_t[head][:, i, u, :].bitcast(BF16).rearrange("p (q e) -> p q e", e=2)[:, :, member],
                    rhs=k_t[head][:, u, key_half * BANK : (key_half + 1) * BANK]
                    .bitcast(BF16)
                    .rearrange("p (n e) -> p n e", e=2)[:, :, member],
                    start=(c == 0),
                    stop=(c == 3),
                )

        def add_bias(j, key_half):
            head, i = divmod(j, TILES)
            h = HEADS[head][1]
            if key_half == 0:
                neg_s[j] = work.tile([P, N], F32, name="neg_s")
            keys = slice(key_half * BANK, (key_half + 1) * BANK)
            nc.vector.scalar_tensor_tensor(
                out=neg_s[j][:, keys],
                in0=score[(j, key_half)][:],
                scalar=neg_factor[:, h : h + 1],
                in1=bias_sb[h][:, i, keys],
                op0=ALU.mult,
                op1=ALU.subtract,
            )

        def row_maximum(j):
            neg_max[j] = columns.tile([P, 1], F32, name="neg_max")
            nc.vector.tensor_reduce(out=neg_max[j][:], in_=neg_s[j][:], axis=AXIS.X, op=ALU.min)

        def exponential(j):
            e_bf[j] = work.tile([P, N], BF16, name="e_bf")
            row_sum[j] = columns.tile([P, 1], F32, name="row_sum")
            nc.scalar.activation(
                out=e_bf[j][:], in_=neg_s[j][:], func=ACT.Exp, bias=neg_max[j][:], scale=-1.0, accum_out=row_sum[j][:]
            )

        def transpose_e(j):
            e_bank[j] = transpose_banks.tile([P, PASSES * PACK, P], BF16, name="e_bank", tag="bank")
            for block in range(PASSES * PACK):
                nc.tensor.transpose(e_bank[j][:, block, :], e_bf[j][:, block * P : (block + 1) * P], identity_bf16[:])

        def regroup_e(j):
            e_grouped[j] = work.tile([P, PASSES, P, PACK], BF16, name="e_grouped", align_bytes=64)
            nc.scalar.copy(out=e_grouped[j][:], in_=e_bank[j][:].rearrange("p (g t) q -> p g q t", t=PACK))

        def quantise_e(j):
            e_words[j] = work.tile([P, PASSES * P], U32, name="e_words", align_bytes=64)
            e_scales[j] = work.tile([P, PASSES * P], U8, name="e_scales", align_bytes=64)
            nc.vector.quantize_mx(
                out=e_words[j][:].bitcast(FP8X4),
                scales=e_scales[j][:],
                in_=e_grouped[j][:].rearrange("p g q t -> p (g q t)"),
            )
            inv_sum[j] = columns.tile([P, 1], F32, name="inv_sum")
            nc.vector.reciprocal(out=inv_sum[j][:], in_=row_sum[j][:])

        def mx_passes(j):
            head = j // TILES
            x_bank[j] = output_banks.tile([P, D], F32, name="x_bank")
            for g in range(PASSES):
                queries = slice(g * P, (g + 1) * P)
                nc.tensor.matmul_mx(
                    out=x_bank[j][:],
                    lhsT=e_words[j][:, queries].bitcast(FP8X4),
                    lhsT_scale=e_scales[j][:, queries],
                    rhs=v_words[head][:, g, :].bitcast(FP8X4),
                    rhs_scale=v_scales[head][:, g, :],
                    start=(g == 0),
                    stop=(g == PASSES - 1),
                )

        def output(j):
            head, i = divmod(j, TILES)
            b, h = HEADS[head]
            x_sb = work.tile([P, D], F32, name="x_sb")
            nc.scalar.activation(out=x_sb[:], in_=x_bank[j][:], func=ACT.Copy, scale=inv_sum[j][:])
            row0 = b * N + i * P
            nc.sync.dma_start(
                out=out_rows[row0 : row0 + P, h : h + 1, :], in_=x_sb[:].rearrange("p (o d) -> p o d", o=1)
            )

        identity_bf16 = const.tile([P, P], BF16, name="identity_bf16")
        make_identity(nc, identity_bf16[:])
        identity_f32 = const.tile([P, P], F32, name="identity_f32")
        make_identity(nc, identity_f32[:])
        log_factor = const.tile([P, NHEADS], BF16, name="log_factor")
        nc.sync.dma_start(out=log_factor[:], in_=logit_scale.rearrange("h a b -> (h a b)").partition_broadcast(P))
        bias_sb = [const.tile([P, TILES, N], BF16, name="bias%d" % h) for h in range(NHEADS)]
        new_head(0)
        load_blocks(k_raw[0], k_rows, first_row(0), 0, 4)
        load_blocks(q_raw[0], q_rows, first_row(0), 0, 2)
        load_blocks(k_raw[0], k_rows, first_row(0), 4, 4)
        load_blocks(bias_sb[0], bias_rows, 0, 0, 1)
        load_blocks(v_raw[0], v_rows, first_row(0), 0, TILES)
        load_blocks(q_raw[0], q_rows, first_row(0), 2, 2)
        load_blocks(bias_sb[0], bias_rows, 0, 1, 1)
        load_blocks(q_raw[0], q_rows, first_row(0), 4, 4)
        load_blocks(bias_sb[0], bias_rows, 0, 2, 2)
        load_blocks(bias_sb[0], bias_rows, 0, 4, 4)

        factor = const.tile([P, NHEADS], F32, name="factor")
        nc.scalar.activation(out=factor[:], in_=log_factor[:], func=ACT.Exp)
        neg_factor = const.tile([P, NHEADS], F32, name="neg_factor")
        nc.vector.tensor_scalar(
            out=neg_factor[:], in0=factor[:], scalar1=100.0, scalar2=-1.0, op0=ALU.min, op1=ALU.mult
        )

        for position, unit in enumerate(UNITS_BEFORE_A_HEAD):
            unit_transposes(0, unit)
            unit_copy(0, unit, on_vector=(position % 2 == 0))
        for piece in range(V_PIECES):
            regroup_v(0, piece)

        def is_tile(j):
            return 0 <= j < ALL_TILES

        for step in range(ALL_TILES + MX_LAG):
            head, i = divmod(step, TILES)
            prepare = head + 1
            preparing = is_tile(step) and prepare < len(HEADS)

            if preparing and i == 0:
                new_head(prepare)
                load_blocks(k_raw[prepare], k_rows, first_row(prepare), 0, TILES)
            if preparing and i == 1:
                load_blocks(q_raw[prepare], q_rows, first_row(prepare), 0, TILES)
            if preparing and i == 2:
                load_blocks(v_raw[prepare], v_rows, first_row(prepare), 0, TILES)
            if step == 3:
                load_blocks(bias_sb[1], bias_rows, N, 0, TILES)

            if i < len(UNITS_IN_A_HEAD):
                unit_head, unit = head, UNITS_IN_A_HEAD[i]
            else:
                unit_head, unit = prepare, UNITS_BEFORE_A_HEAD[i - len(UNITS_IN_A_HEAD)]
            has_unit = is_tile(step) and unit_head < len(HEADS)

            if is_tile(step):
                scores(step, 0)
            if is_tile(step - MX_LAG):
                mx_passes(step - MX_LAG)
            if is_tile(step):
                scores(step, 1)
            if is_tile(step - TRANSPOSE_LAG):
                transpose_e(step - TRANSPOSE_LAG)
            if has_unit:
                unit_transposes(unit_head, unit)

            if is_tile(step):
                add_bias(step, 0)
            if is_tile(step - QUANTISE_LAG):
                quantise_e(step - QUANTISE_LAG)
            if is_tile(step):
                add_bias(step, 1)
                row_maximum(step)
            if step == MX_LAG - 2:
                quantise_v(0)
            if preparing and i == TILES - 1:
                quantise_v(prepare)

            if is_tile(step - EXP_LAG):
                exponential(step - EXP_LAG)
            if is_tile(step - MX_LAG):
                output(step - MX_LAG)
            if is_tile(step - TRANSPOSE_LAG):
                regroup_e(step - TRANSPOSE_LAG)
            if has_unit:
                unit_copy(unit_head, unit, on_vector=False)

            first_piece = (i - V_FIRST_STEP) * V_PIECES_A_STEP
            if preparing and 0 <= first_piece < V_PIECES:
                for piece in range(first_piece, first_piece + V_PIECES_A_STEP):
                    regroup_v(prepare, piece)
